import numpy as np
import ml_dtypes

BF16 = ml_dtypes.bfloat16


def bf(x):
    return np.asarray(x, np.float32).astype(BF16)


def f32(x):
    return np.asarray(x, np.float32)


def f64(x):
    return np.asarray(x).astype(np.float64)


def striped(idx):
    return np.tile(idx.reshape(-1, 16).T, (8, 1))


S, D, M, N, K = 4096, 128, 128, 4096, 8


def setup_inputs():
    return {"table": bf(np.random.standard_normal((S, D))),
            "w1": bf(np.random.standard_normal((D, M)) / np.sqrt(D)),
            "b1": f32(0.1 * np.random.standard_normal((M, 1))),
            "w2": bf(np.random.standard_normal((M, M)) / np.sqrt(M)),
            "b2": f32(0.1 * np.random.standard_normal((M, 1))),
            "w3": bf(np.random.standard_normal((M, M)) / np.sqrt(M)),
            "b3": f32(0.1 * np.random.standard_normal((M, 1))),
            "offs": striped(np.random.permutation(S)[:N])}


def reference(table, w1, b1, w2, b2, w3, b3, offs):
    idx = offs[:16].T.reshape(-1)
    h = np.maximum(f64(w1).T @ f64(table)[idx].T + f64(b1), 0.0)
    h = np.maximum(f64(w2).T @ h + f64(b2), 0.0)
    h = np.maximum(f64(w3).T @ h + f64(b3), 0.0)
    return h.reshape(M, N // K, K).max(axis=-1)

@@ -1,0 +1,86 @@
+import concourse.mybir as mybir
+from concourse.masks import make_identity
+
+BF16, F32, U16 = mybir.dt.bfloat16, mybir.dt.float32, mybir.dt.uint16
+ADD, MAX = mybir.AluOpType.add, mybir.AluOpType.max
+RELU = mybir.ActivationFunctionType.Relu
+
+P = 128
+POINTS = 4096
+ENTRIES = 4096
+BALL = 8
+PIECE = 512
+N_PIECES = ENTRIES // PIECE
+BLOCKS = POINTS // P
+GROUP = 4
+
+FLOPS = 2 * ENTRIES * P * P * 3
+
+
+def tile_setabstraction_kernel(tc, table, w1, b1, w2, b2, w3, b3, offs, out):
+    nc = tc.nc
+    with (
+        tc.tile_pool(name="held", bufs=1) as held,
+        tc.tile_pool(name="acts", bufs=3) as acts,
+        tc.psum_pool(name="psum", bufs=8) as psum,
+    ):
+        identity = held.tile([P, P], BF16, name="identity")
+        make_identity(nc, identity[:])
+
+        offsets = held.tile([P, ENTRIES // 16], U16, name="offsets")
+        nc.sync.dma_start(offsets[:], offs)
+
+        weights = [held.tile([P, P], BF16, name=f"w{layer}") for layer in range(3)]
+        biases = [held.tile([P, 1], F32, name=f"b{layer}") for layer in range(3)]
+        nc.scalar.dma_start(weights[0][:], w1)
+        for b_tile, b in zip(biases, (b1, b2, b3)):
+            nc.gpsimd.dma_start(b_tile[:], b)
+
+        rows = held.tile([P, BLOCKS, P], BF16, name="rows")
+        table_blocks = table.rearrange("(n p) d -> p n d", p=P)
+        for g in range(BLOCKS // GROUP):
+            queue = nc.sync if g % 2 == 0 else nc.scalar
+            blocks = slice(g * GROUP, (g + 1) * GROUP)
+            queue.dma_start(rows[:, blocks, :], table_blocks[:, blocks, :])
+
+        nc.sync.dma_start(weights[1][:], w2)
+        nc.scalar.dma_start(weights[2][:], w3)
+
+        window = held.tile([P, POINTS], BF16, name="window")
+        for g in range(BLOCKS // GROUP):
+            flipped = psum.tile([P, GROUP * P], BF16, name="flipped", tag="bank")
+            for k in range(GROUP):
+                nc.tensor.transpose(flipped[:, k * P : (k + 1) * P], rows[:, g * GROUP + k, :], identity[:])
+            columns = slice(g * GROUP * P, (g + 1) * GROUP * P)
+            if g % 2 == 0:
+                nc.vector.tensor_copy(window[:, columns], flipped[:])
+            else:
+                nc.scalar.copy(window[:, columns], flipped[:])
+
+        h1 = held.tile([P, N_PIECES, PIECE], BF16, name="h1")
+        for i in range(N_PIECES):
+            sum1 = psum.tile([P, PIECE], F32, name="sum1", tag="bank")
+            looked_up = window[:].indirect(offsets[:, i * (PIECE // 16) : (i + 1) * (PIECE // 16)])
+            nc.tensor.matmul(sum1[:], weights[0][:], looked_up, start=True, stop=True)
+            if i % 2 == 0:
+                nc.scalar.activation(h1[:, i, :], sum1[:], RELU, bias=biases[0][:])
+            else:
+                nc.vector.tensor_scalar(h1[:, i, :], sum1[:], biases[0][:], 0.0, ADD, MAX)
+
+        pooled = held.tile([P, ENTRIES // BALL], F32, name="pooled")
+        for i in range(N_PIECES):
+            sum2 = psum.tile([P, PIECE], F32, name="sum2", tag="bank")
+            nc.tensor.matmul(sum2[:], weights[1][:], h1[:, i, :], start=True, stop=True)
+            h2 = acts.tile([P, PIECE], BF16, name="h2")
+            nc.scalar.activation(h2[:], sum2[:], RELU, bias=biases[1][:])
+
+            sum3 = psum.tile([P, PIECE], F32, name="sum3", tag="bank")
+            nc.tensor.matmul(sum3[:], weights[2][:], h2[:], start=True, stop=True)
+            balls = slice(i * (PIECE // BALL), (i + 1) * (PIECE // BALL))
+            nc.vector.tensor_reduce(
+                pooled[:, balls], sum3[:].rearrange("r (q k) -> r q k", k=BALL), mybir.AxisListType.X, MAX
+            )
+
+        result = held.tile([P, ENTRIES // BALL], F32, name="result")
+        nc.vector.tensor_scalar(result[:], pooled[:], biases[2][:], 0.0, ADD, MAX)
+        nc.sync.dma_start(out, result[:])

@@ -13,6 +13,7 @@ PIECE = 512
 N_PIECES = ENTRIES // PIECE
 BLOCKS = POINTS // P
 GROUP = 4
+LAG = 2
 
 FLOPS = 2 * ENTRIES * P * P * 3
 
@@ -21,7 +22,6 @@ def tile_setabstraction_kernel(tc, table, w1, b1, w2, b2, w3, b3, offs, out):
     nc = tc.nc
     with (
         tc.tile_pool(name="held", bufs=1) as held,
-        tc.tile_pool(name="acts", bufs=3) as acts,
         tc.psum_pool(name="psum", bufs=8) as psum,
     ):
         identity = held.tile([P, P], BF16, name="identity")
@@ -46,6 +46,10 @@ def tile_setabstraction_kernel(tc, table, w1, b1, w2, b2, w3, b3, offs, out):
         nc.sync.dma_start(weights[1][:], w2)
         nc.scalar.dma_start(weights[2][:], w3)
 
+        scratch = held.tile([P, 1], F32, name="scratch")
+        nc.vector.memset(scratch[:], 0.0)
+        nc.scalar.activation(scratch[:], scratch[:], RELU)
+
         window = held.tile([P, POINTS], BF16, name="window")
         for g in range(BLOCKS // GROUP):
             flipped = psum.tile([P, GROUP * P], BF16, name="flipped", tag="bank")
@@ -67,19 +71,22 @@ def tile_setabstraction_kernel(tc, table, w1, b1, w2, b2, w3, b3, offs, out):
             else:
                 nc.vector.tensor_scalar(h1[:, i, :], sum1[:], biases[0][:], 0.0, ADD, MAX)
 
+        h2 = held.tile([P, N_PIECES, PIECE], BF16, name="h2")
         pooled = held.tile([P, ENTRIES // BALL], F32, name="pooled")
-        for i in range(N_PIECES):
-            sum2 = psum.tile([P, PIECE], F32, name="sum2", tag="bank")
-            nc.tensor.matmul(sum2[:], weights[1][:], h1[:, i, :], start=True, stop=True)
-            h2 = acts.tile([P, PIECE], BF16, name="h2")
-            nc.scalar.activation(h2[:], sum2[:], RELU, bias=biases[1][:])
-
-            sum3 = psum.tile([P, PIECE], F32, name="sum3", tag="bank")
-            nc.tensor.matmul(sum3[:], weights[2][:], h2[:], start=True, stop=True)
-            balls = slice(i * (PIECE // BALL), (i + 1) * (PIECE // BALL))
-            nc.vector.tensor_reduce(
-                pooled[:, balls], sum3[:].rearrange("r (q k) -> r q k", k=BALL), mybir.AxisListType.X, MAX
-            )
+        for step in range(N_PIECES + LAG):
+            if step < N_PIECES:
+                i = step
+                sum2 = psum.tile([P, PIECE], F32, name="sum2", tag="bank")
+                nc.tensor.matmul(sum2[:], weights[1][:], h1[:, i, :], start=True, stop=True)
+                nc.scalar.activation(h2[:, i, :], sum2[:], RELU, bias=biases[1][:])
+            if step >= LAG:
+                i = step - LAG
+                sum3 = psum.tile([P, PIECE], F32, name="sum3", tag="bank")
+                nc.tensor.matmul(sum3[:], weights[2][:], h2[:, i, :], start=True, stop=True)
+                balls = slice(i * (PIECE // BALL), (i + 1) * (PIECE // BALL))
+                nc.vector.tensor_reduce(
+                    pooled[:, balls], sum3[:].rearrange("r (q k) -> r q k", k=BALL), mybir.AxisListType.X, MAX
+                )
 
         result = held.tile([P, ENTRIES // BALL], F32, name="result")
         nc.vector.tensor_scalar(result[:], pooled[:], biases[2][:], 0.0, ADD, MAX)

@@ -13,6 +13,7 @@ PIECE = 512
 N_PIECES = ENTRIES // PIECE
 BLOCKS = POINTS // P
 GROUP = 4
+WARM_UP = 5
 LAG = 2
 
 FLOPS = 2 * ENTRIES * P * P * 3
@@ -24,6 +25,16 @@ def tile_setabstraction_kernel(tc, table, w1, b1, w2, b2, w3, b3, offs, out):
         tc.tile_pool(name="held", bufs=1) as held,
         tc.psum_pool(name="psum", bufs=8) as psum,
     ):
+        zeros = held.tile([P, PIECE], BF16, name="zeros")
+        nc.vector.memset(zeros[:], 0.0)
+
+        def idle_matmul():
+            unread = psum.tile([P, PIECE], F32, name="unread", tag="bank")
+            nc.tensor.matmul(unread[:], zeros[:, :P], zeros[:], start=True, stop=True)
+
+        for n in range(WARM_UP):
+            idle_matmul()
+
         identity = held.tile([P, P], BF16, name="identity")
         make_identity(nc, identity[:])
 
@@ -60,6 +71,7 @@ def tile_setabstraction_kernel(tc, table, w1, b1, w2, b2, w3, b3, offs, out):
                 nc.vector.tensor_copy(window[:, columns], flipped[:])
             else:
                 nc.scalar.copy(window[:, columns], flipped[:])
+                idle_matmul()
 
         h1 = held.tile([P, N_PIECES, PIECE], BF16, name="h1")
         for i in range(N_PIECES):

@@ -11,8 +11,8 @@ ENTRIES = 4096
 BALL = 8
 PIECE = 512
 N_PIECES = ENTRIES // PIECE
-BLOCKS = POINTS // P
 GROUP = 4
+N_GROUPS = POINTS // (GROUP * P)
 WARM_UP = 5
 LAG = 2
 
@@ -38,39 +38,35 @@ def tile_setabstraction_kernel(tc, table, w1, b1, w2, b2, w3, b3, offs, out):
         identity = held.tile([P, P], BF16, name="identity")
         make_identity(nc, identity[:])
 
+        rows = held.tile([P, N_GROUPS, GROUP, P], BF16, name="rows")
+        table_groups = table.rearrange("(g p j) d -> p g j d", p=P, j=GROUP)
+        for g in range(N_GROUPS):
+            queue = nc.sync if g % 2 == 0 else nc.scalar
+            queue.dma_start(rows[:, g, :, :], table_groups[:, g, :, :])
+
         offsets = held.tile([P, ENTRIES // 16], U16, name="offsets")
         nc.sync.dma_start(offsets[:], offs)
-
         weights = [held.tile([P, P], BF16, name=f"w{layer}") for layer in range(3)]
         biases = [held.tile([P, 1], F32, name=f"b{layer}") for layer in range(3)]
-        nc.scalar.dma_start(weights[0][:], w1)
-        for b_tile, b in zip(biases, (b1, b2, b3)):
-            nc.gpsimd.dma_start(b_tile[:], b)
-
-        rows = held.tile([P, BLOCKS, P], BF16, name="rows")
-        table_blocks = table.rearrange("(n p) d -> p n d", p=P)
-        for g in range(BLOCKS // GROUP):
-            queue = nc.sync if g % 2 == 0 else nc.scalar
-            blocks = slice(g * GROUP, (g + 1) * GROUP)
-            queue.dma_start(rows[:, blocks, :], table_blocks[:, blocks, :])
-
-        nc.sync.dma_start(weights[1][:], w2)
-        nc.scalar.dma_start(weights[2][:], w3)
+        for w_tile, w, b_tile, b in zip(weights, (w1, w2, w3), biases, (b1, b2, b3)):
+            nc.sync.dma_start(w_tile[:], w)
+            nc.sync.dma_start(b_tile[:], b)
 
         scratch = held.tile([P, 1], F32, name="scratch")
         nc.vector.memset(scratch[:], 0.0)
         nc.scalar.activation(scratch[:], scratch[:], RELU)
 
         window = held.tile([P, POINTS], BF16, name="window")
-        for g in range(BLOCKS // GROUP):
-            flipped = psum.tile([P, GROUP * P], BF16, name="flipped", tag="bank")
-            for k in range(GROUP):
-                nc.tensor.transpose(flipped[:, k * P : (k + 1) * P], rows[:, g * GROUP + k, :], identity[:])
-            columns = slice(g * GROUP * P, (g + 1) * GROUP * P)
+        for g in range(N_GROUPS):
+            flipped = psum.tile([P, GROUP, P], BF16, name="flipped", tag="bank")
+            for j in range(GROUP):
+                nc.tensor.transpose(flipped[:, j, :], rows[:, g, j, :], identity[:])
+            columns = window[:, g * GROUP * P : (g + 1) * GROUP * P].rearrange("d (p j) -> d p j", j=GROUP)
+            in_point_order = flipped[:].rearrange("d j p -> d p j")
             if g % 2 == 0:
-                nc.vector.tensor_copy(window[:, columns], flipped[:])
+                nc.vector.tensor_copy(columns, in_point_order)
             else:
-                nc.scalar.copy(window[:, columns], flipped[:])
+                nc.scalar.copy(columns, in_point_order)
                 idle_matmul()
 
         h1 = held.tile([P, N_PIECES, PIECE], BF16, name="h1")
@@ -90,7 +86,10 @@ def tile_setabstraction_kernel(tc, table, w1, b1, w2, b2, w3, b3, offs, out):
                 i = step
                 sum2 = psum.tile([P, PIECE], F32, name="sum2", tag="bank")
                 nc.tensor.matmul(sum2[:], weights[1][:], h1[:, i, :], start=True, stop=True)
-                nc.scalar.activation(h2[:, i, :], sum2[:], RELU, bias=biases[1][:])
+                if i % 2 == 1 and i < 2 * LAG:
+                    nc.vector.tensor_scalar(h2[:, i, :], sum2[:], biases[1][:], 0.0, ADD, MAX)
+                else:
+                    nc.scalar.activation(h2[:, i, :], sum2[:], RELU, bias=biases[1][:])
             if step >= LAG:
                 i = step - LAG
                 sum3 = psum.tile([P, PIECE], F32, name="sum3", tag="bank")
@@ -101,5 +100,8 @@ def tile_setabstraction_kernel(tc, table, w1, b1, w2, b2, w3, b3, offs, out):
                 )
 
         result = held.tile([P, ENTRIES // BALL], F32, name="result")
-        nc.vector.tensor_scalar(result[:], pooled[:], biases[2][:], 0.0, ADD, MAX)
-        nc.sync.dma_start(out, result[:])
+        early = (N_PIECES - LAG) * (PIECE // BALL)
+        nc.scalar.activation(result[:, :early], pooled[:, :early], RELU, bias=biases[2][:])
+        nc.scalar.dma_start(out[:, :early], result[:, :early])
+        nc.vector.tensor_scalar(result[:, early:], pooled[:, early:], biases[2][:], 0.0, ADD, MAX)
+        nc.sync.dma_start(out[:, early:], result[:, early:])

@@ -13,8 +13,9 @@ PIECE = 512
 N_PIECES = ENTRIES // PIECE
 GROUP = 4
 N_GROUPS = POINTS // (GROUP * P)
-WARM_UP = 5
-LAG = 2
+WARM_UP = 3
+LAG = 3
+LAST = 2
 
 FLOPS = 2 * ENTRIES * P * P * 3
 
@@ -40,17 +41,21 @@ def tile_setabstraction_kernel(tc, table, w1, b1, w2, b2, w3, b3, offs, out):
 
         rows = held.tile([P, N_GROUPS, GROUP, P], BF16, name="rows")
         table_groups = table.rearrange("(g p j) d -> p g j d", p=P, j=GROUP)
-        for g in range(N_GROUPS):
-            queue = nc.sync if g % 2 == 0 else nc.scalar
-            queue.dma_start(rows[:, g, :, :], table_groups[:, g, :, :])
-
+        first_group = 0
+        for n, groups in enumerate((2, 2, 2, 1, 1)):
+            queue = nc.sync if n % 2 == 0 else nc.scalar
+            loaded = slice(first_group, first_group + groups)
+            queue.dma_start(rows[:, loaded, :, :], table_groups[:, loaded, :, :])
+            first_group += groups
         offsets = held.tile([P, ENTRIES // 16], U16, name="offsets")
         nc.sync.dma_start(offsets[:], offs)
         weights = [held.tile([P, P], BF16, name=f"w{layer}") for layer in range(3)]
         biases = [held.tile([P, 1], F32, name=f"b{layer}") for layer in range(3)]
-        for w_tile, w, b_tile, b in zip(weights, (w1, w2, w3), biases, (b1, b2, b3)):
-            nc.sync.dma_start(w_tile[:], w)
-            nc.sync.dma_start(b_tile[:], b)
+        nc.scalar.dma_start(weights[0][:], w1)
+        nc.scalar.dma_start(biases[0][:], b1)
+        for layer, (w, b) in enumerate(((w2, b2), (w3, b3)), start=1):
+            nc.sync.dma_start(weights[layer][:], w)
+            nc.sync.dma_start(biases[layer][:], b)
 
         scratch = held.tile([P, 1], F32, name="scratch")
         nc.vector.memset(scratch[:], 0.0)
@@ -86,7 +91,7 @@ def tile_setabstraction_kernel(tc, table, w1, b1, w2, b2, w3, b3, offs, out):
                 i = step
                 sum2 = psum.tile([P, PIECE], F32, name="sum2", tag="bank")
                 nc.tensor.matmul(sum2[:], weights[1][:], h1[:, i, :], start=True, stop=True)
-                if i % 2 == 1 and i < 2 * LAG:
+                if i == 1:
                     nc.vector.tensor_scalar(h2[:, i, :], sum2[:], biases[1][:], 0.0, ADD, MAX)
                 else:
                     nc.scalar.activation(h2[:, i, :], sum2[:], RELU, bias=biases[1][:])
@@ -100,7 +105,7 @@ def tile_setabstraction_kernel(tc, table, w1, b1, w2, b2, w3, b3, offs, out):
                 )
 
         result = held.tile([P, ENTRIES // BALL], F32, name="result")
-        early = (N_PIECES - LAG) * (PIECE // BALL)
+        early = (N_PIECES - LAST) * (PIECE // BALL)
         nc.scalar.activation(result[:, :early], pooled[:, :early], RELU, bias=biases[2][:])
         nc.scalar.dma_start(out[:, :early], result[:, :early])
         nc.vector.tensor_scalar(result[:, early:], pooled[:, early:], biases[2][:], 0.0, ADD, MAX)

@@ -41,18 +41,14 @@ def tile_setabstraction_kernel(tc, table, w1, b1, w2, b2, w3, b3, offs, out):
 
         rows = held.tile([P, N_GROUPS, GROUP, P], BF16, name="rows")
         table_groups = table.rearrange("(g p j) d -> p g j d", p=P, j=GROUP)
-        first_group = 0
-        for n, groups in enumerate((2, 2, 2, 1, 1)):
-            queue = nc.sync if n % 2 == 0 else nc.scalar
-            loaded = slice(first_group, first_group + groups)
-            queue.dma_start(rows[:, loaded, :, :], table_groups[:, loaded, :, :])
-            first_group += groups
+        for g in range(N_GROUPS):
+            nc.sync.dma_start(rows[:, g, :, :], table_groups[:, g, :, :])
         offsets = held.tile([P, ENTRIES // 16], U16, name="offsets")
         nc.sync.dma_start(offsets[:], offs)
         weights = [held.tile([P, P], BF16, name=f"w{layer}") for layer in range(3)]
         biases = [held.tile([P, 1], F32, name=f"b{layer}") for layer in range(3)]
-        nc.scalar.dma_start(weights[0][:], w1)
-        nc.scalar.dma_start(biases[0][:], b1)
+        nc.gpsimd.dma_start(weights[0][:], w1)
+        nc.gpsimd.dma_start(biases[0][:], b1)
         for layer, (w, b) in enumerate(((w2, b2), (w3, b3)), start=1):
             nc.sync.dma_start(weights[layer][:], w)
             nc.sync.dma_start(biases[layer][:], b)

@@ -13,8 +13,10 @@ PIECE = 512
 N_PIECES = ENTRIES // PIECE
 GROUP = 4
 N_GROUPS = POINTS // (GROUP * P)
+UNITS = (2,) + (1,) * (N_GROUPS - 2) + (2,)
 WARM_UP = 3
-LAG = 3
+CHUNKS = (PIECE // 4, 3 * PIECE // 4) + (PIECE,) * (N_PIECES - 1)
+LAG = 2
 LAST = 2
 
 FLOPS = 2 * ENTRIES * P * P * 3
@@ -40,9 +42,12 @@ def tile_setabstraction_kernel(tc, table, w1, b1, w2, b2, w3, b3, offs, out):
         make_identity(nc, identity[:])
 
         rows = held.tile([P, N_GROUPS, GROUP, P], BF16, name="rows")
-        table_groups = table.rearrange("(g p j) d -> p g j d", p=P, j=GROUP)
         for g in range(N_GROUPS):
-            nc.sync.dma_start(rows[:, g, :, :], table_groups[:, g, :, :])
+            group_points = table[g * GROUP * P : (g + 1) * GROUP * P, :]
+            nc.sync.dma_start(
+                rows[:, g, :, :].rearrange("p (u j) d -> p u j d", u=UNITS[g]),
+                group_points.rearrange("(u p j) d -> p u j d", u=UNITS[g], p=P),
+            )
         offsets = held.tile([P, ENTRIES // 16], U16, name="offsets")
         nc.sync.dma_start(offsets[:], offs)
         weights = [held.tile([P, P], BF16, name=f"w{layer}") for layer in range(3)]
@@ -58,46 +63,51 @@ def tile_setabstraction_kernel(tc, table, w1, b1, w2, b2, w3, b3, offs, out):
         nc.scalar.activation(scratch[:], scratch[:], RELU)
 
         window = held.tile([P, POINTS], BF16, name="window")
+        n_units = 0
         for g in range(N_GROUPS):
-            flipped = psum.tile([P, GROUP, P], BF16, name="flipped", tag="bank")
-            for j in range(GROUP):
-                nc.tensor.transpose(flipped[:, j, :], rows[:, g, j, :], identity[:])
-            columns = window[:, g * GROUP * P : (g + 1) * GROUP * P].rearrange("d (p j) -> d p j", j=GROUP)
-            in_point_order = flipped[:].rearrange("d j p -> d p j")
-            if g % 2 == 0:
-                nc.vector.tensor_copy(columns, in_point_order)
-            else:
-                nc.scalar.copy(columns, in_point_order)
+            blocks = GROUP // UNITS[g]
+            for u in range(UNITS[g]):
+                flipped = psum.tile([P, blocks, P], BF16, name="flipped", tag="bank")
+                for j in range(blocks):
+                    nc.tensor.transpose(flipped[:, j, :], rows[:, g, u * blocks + j, :], identity[:])
+                first = (g * GROUP + u * blocks) * P
+                columns = window[:, first : first + blocks * P].rearrange("d (p j) -> d p j", j=blocks)
+                in_point_order = flipped[:].rearrange("d j p -> d p j")
+                if n_units % 2 == 0:
+                    nc.vector.tensor_copy(columns, in_point_order)
+                else:
+                    nc.scalar.copy(columns, in_point_order)
+                n_units += 1
+            if g % 2 == 1:
                 idle_matmul()
 
-        h1 = held.tile([P, N_PIECES, PIECE], BF16, name="h1")
+        h1 = held.tile([P, ENTRIES], BF16, name="h1")
         for i in range(N_PIECES):
             sum1 = psum.tile([P, PIECE], F32, name="sum1", tag="bank")
             looked_up = window[:].indirect(offsets[:, i * (PIECE // 16) : (i + 1) * (PIECE // 16)])
             nc.tensor.matmul(sum1[:], weights[0][:], looked_up, start=True, stop=True)
+            piece = slice(i * PIECE, (i + 1) * PIECE)
             if i % 2 == 0:
-                nc.scalar.activation(h1[:, i, :], sum1[:], RELU, bias=biases[0][:])
+                nc.scalar.activation(h1[:, piece], sum1[:], RELU, bias=biases[0][:])
             else:
-                nc.vector.tensor_scalar(h1[:, i, :], sum1[:], biases[0][:], 0.0, ADD, MAX)
+                nc.vector.tensor_scalar(h1[:, piece], sum1[:], biases[0][:], 0.0, ADD, MAX)
 
-        h2 = held.tile([P, N_PIECES, PIECE], BF16, name="h2")
+        h2 = held.tile([P, ENTRIES], BF16, name="h2")
         pooled = held.tile([P, ENTRIES // BALL], F32, name="pooled")
-        for step in range(N_PIECES + LAG):
-            if step < N_PIECES:
-                i = step
+        chunk_entries = [slice(sum(CHUNKS[:c]), sum(CHUNKS[: c + 1])) for c in range(len(CHUNKS))]
+        for step in range(len(CHUNKS) + LAG):
+            if step < len(CHUNKS):
+                entries, width = chunk_entries[step], CHUNKS[step]
                 sum2 = psum.tile([P, PIECE], F32, name="sum2", tag="bank")
-                nc.tensor.matmul(sum2[:], weights[1][:], h1[:, i, :], start=True, stop=True)
-                if i == 1:
-                    nc.vector.tensor_scalar(h2[:, i, :], sum2[:], biases[1][:], 0.0, ADD, MAX)
-                else:
-                    nc.scalar.activation(h2[:, i, :], sum2[:], RELU, bias=biases[1][:])
+                nc.tensor.matmul(sum2[:, :width], weights[1][:], h1[:, entries], start=True, stop=True)
+                nc.scalar.activation(h2[:, entries], sum2[:, :width], RELU, bias=biases[1][:])
             if step >= LAG:
-                i = step - LAG
+                entries, width = chunk_entries[step - LAG], CHUNKS[step - LAG]
                 sum3 = psum.tile([P, PIECE], F32, name="sum3", tag="bank")
-                nc.tensor.matmul(sum3[:], weights[2][:], h2[:, i, :], start=True, stop=True)
-                balls = slice(i * (PIECE // BALL), (i + 1) * (PIECE // BALL))
+                nc.tensor.matmul(sum3[:, :width], weights[2][:], h2[:, entries], start=True, stop=True)
+                balls = slice(entries.start // BALL, entries.stop // BALL)
                 nc.vector.tensor_reduce(
-                    pooled[:, balls], sum3[:].rearrange("r (q k) -> r q k", k=BALL), mybir.AxisListType.X, MAX
+                    pooled[:, balls], sum3[:, :width].rearrange("r (q k) -> r q k", k=BALL), mybir.AxisListType.X, MAX
                 )
 
         result = held.tile([P, ENTRIES // BALL], F32, name="result")

@@ -15,8 +15,8 @@ GROUP = 4
 N_GROUPS = POINTS // (GROUP * P)
 UNITS = (2,) + (1,) * (N_GROUPS - 2) + (2,)
 WARM_UP = 3
-CHUNKS = (PIECE // 4, 3 * PIECE // 4) + (PIECE,) * (N_PIECES - 1)
-LAG = 2
+CHUNKS = (PIECE // 2,) * (2 * N_PIECES)
+LAG = 3
 LAST = 2
 
 FLOPS = 2 * ENTRIES * P * P * 3

import concourse.mybir as mybir
from concourse.masks import make_identity

BF16, F32, U16 = mybir.dt.bfloat16, mybir.dt.float32, mybir.dt.uint16
ADD, MAX = mybir.AluOpType.add, mybir.AluOpType.max
RELU = mybir.ActivationFunctionType.Relu

P = 128
POINTS = 4096
ENTRIES = 4096
BALL = 8
PIECE = 512
N_PIECES = ENTRIES // PIECE
GROUP = 4
N_GROUPS = POINTS // (GROUP * P)
UNITS = (2,) + (1,) * (N_GROUPS - 2) + (2,)
WARM_UP = 3
CHUNKS = (PIECE // 2,) * (2 * N_PIECES)
LAG = 3
LAST = 2

FLOPS = 2 * ENTRIES * P * P * 3


def tile_setabstraction_kernel(tc, table, w1, b1, w2, b2, w3, b3, offs, out):
    nc = tc.nc
    with (
        tc.tile_pool(name="held", bufs=1) as held,
        tc.psum_pool(name="psum", bufs=8) as psum,
    ):
        zeros = held.tile([P, PIECE], BF16, name="zeros")
        nc.vector.memset(zeros[:], 0.0)

        def idle_matmul():
            unread = psum.tile([P, PIECE], F32, name="unread", tag="bank")
            nc.tensor.matmul(unread[:], zeros[:, :P], zeros[:], start=True, stop=True)

        for n in range(WARM_UP):
            idle_matmul()

        identity = held.tile([P, P], BF16, name="identity")
        make_identity(nc, identity[:])

        rows = held.tile([P, N_GROUPS, GROUP, P], BF16, name="rows")
        for g in range(N_GROUPS):
            group_points = table[g * GROUP * P : (g + 1) * GROUP * P, :]
            nc.sync.dma_start(
                rows[:, g, :, :].rearrange("p (u j) d -> p u j d", u=UNITS[g]),
                group_points.rearrange("(u p j) d -> p u j d", u=UNITS[g], p=P),
            )
        offsets = held.tile([P, ENTRIES // 16], U16, name="offsets")
        nc.sync.dma_start(offsets[:], offs)
        weights = [held.tile([P, P], BF16, name=f"w{layer}") for layer in range(3)]
        biases = [held.tile([P, 1], F32, name=f"b{layer}") for layer in range(3)]
        nc.gpsimd.dma_start(weights[0][:], w1)
        nc.gpsimd.dma_start(biases[0][:], b1)
        for layer, (w, b) in enumerate(((w2, b2), (w3, b3)), start=1):
            nc.sync.dma_start(weights[layer][:], w)
            nc.sync.dma_start(biases[layer][:], b)

        scratch = held.tile([P, 1], F32, name="scratch")
        nc.vector.memset(scratch[:], 0.0)
        nc.scalar.activation(scratch[:], scratch[:], RELU)

        window = held.tile([P, POINTS], BF16, name="window")
        n_units = 0
        for g in range(N_GROUPS):
            blocks = GROUP // UNITS[g]
            for u in range(UNITS[g]):
                flipped = psum.tile([P, blocks, P], BF16, name="flipped", tag="bank")
                for j in range(blocks):
                    nc.tensor.transpose(flipped[:, j, :], rows[:, g, u * blocks + j, :], identity[:])
                first = (g * GROUP + u * blocks) * P
                columns = window[:, first : first + blocks * P].rearrange("d (p j) -> d p j", j=blocks)
                in_point_order = flipped[:].rearrange("d j p -> d p j")
                if n_units % 2 == 0:
                    nc.vector.tensor_copy(columns, in_point_order)
                else:
                    nc.scalar.copy(columns, in_point_order)
                n_units += 1
            if g % 2 == 1:
                idle_matmul()

        h1 = held.tile([P, ENTRIES], BF16, name="h1")
        for i in range(N_PIECES):
            sum1 = psum.tile([P, PIECE], F32, name="sum1", tag="bank")
            looked_up = window[:].indirect(offsets[:, i * (PIECE // 16) : (i + 1) * (PIECE // 16)])
            nc.tensor.matmul(sum1[:], weights[0][:], looked_up, start=True, stop=True)
            piece = slice(i * PIECE, (i + 1) * PIECE)
            if i % 2 == 0:
                nc.scalar.activation(h1[:, piece], sum1[:], RELU, bias=biases[0][:])
            else:
                nc.vector.tensor_scalar(h1[:, piece], sum1[:], biases[0][:], 0.0, ADD, MAX)

        h2 = held.tile([P, ENTRIES], BF16, name="h2")
        pooled = held.tile([P, ENTRIES // BALL], F32, name="pooled")
        chunk_entries = [slice(sum(CHUNKS[:c]), sum(CHUNKS[: c + 1])) for c in range(len(CHUNKS))]
        for step in range(len(CHUNKS) + LAG):
            if step < len(CHUNKS):
                entries, width = chunk_entries[step], CHUNKS[step]
                sum2 = psum.tile([P, PIECE], F32, name="sum2", tag="bank")
                nc.tensor.matmul(sum2[:, :width], weights[1][:], h1[:, entries], start=True, stop=True)
                nc.scalar.activation(h2[:, entries], sum2[:, :width], RELU, bias=biases[1][:])
            if step >= LAG:
                entries, width = chunk_entries[step - LAG], CHUNKS[step - LAG]
                sum3 = psum.tile([P, PIECE], F32, name="sum3", tag="bank")
                nc.tensor.matmul(sum3[:, :width], weights[2][:], h2[:, entries], start=True, stop=True)
                balls = slice(entries.start // BALL, entries.stop // BALL)
                nc.vector.tensor_reduce(
                    pooled[:, balls], sum3[:, :width].rearrange("r (q k) -> r q k", k=BALL), mybir.AxisListType.X, MAX
                )

        result = held.tile([P, ENTRIES // BALL], F32, name="result")
        early = (N_PIECES - LAST) * (PIECE // BALL)
        nc.scalar.activation(result[:, :early], pooled[:, :early], RELU, bias=biases[2][:])
        nc.scalar.dma_start(out[:, :early], result[:, :early])
        nc.vector.tensor_scalar(result[:, early:], pooled[:, early:], biases[2][:], 0.0, ADD, MAX)
        nc.sync.dma_start(out[:, early:], result[:, early:])
